import numpy as np
import ml_dtypes


def mxq(x, axis, fmt="e4m3"):
    dtype, down = {"e4m3": (ml_dtypes.float8_e4m3fn, 7), "e5m2": (ml_dtypes.float8_e5m2, 14)}[fmt]
    v = np.moveaxis(np.asarray(x, np.float32).astype(ml_dtypes.bfloat16).astype(np.float64), axis, -1)
    blocks = v.reshape(v.shape[:-1] + (-1, 32))
    amax = np.abs(blocks).max(-1, keepdims=True)
    byte = np.maximum(np.where(amax > 0, np.frexp(amax)[1] - 1 + 127, 0) - down, 1)
    scale = np.exp2(byte - 127.0)
    codes = (blocks / scale).astype(np.float32).astype(dtype).astype(np.float64)
    return np.moveaxis((codes * scale).reshape(v.shape), -1, axis)


WIDE = False


def mx_kscale(k):
    if not WIDE:
        return np.ones(k)
    levels = np.array([10, -10, 5, -5, 0])
    a = np.random.permutation(np.resize(levels, k // 512 * 4)).reshape(k // 512, 4)
    idx = np.arange(k)
    return np.exp2(a[idx // 512, idx % 128 // 32])


BF16 = ml_dtypes.bfloat16


def bf(x):
    return np.asarray(x, np.float32).astype(BF16)


def f64(x):
    return np.asarray(x).astype(np.float64)


B, NP, H, W, EMB = 2, 128, 16, 24, 256
L = NP + H * W
C2 = EMB + EMB
BN_EPS = 1e-5


def setup_inputs():
    s = mx_kscale(C2)
    return {'T1': bf(np.random.standard_normal((B, L, EMB)) * s[:EMB]),
            'T2': bf(np.random.standard_normal((B, L, EMB)) * s[EMB:]),
            'Wf': bf(np.random.standard_normal((EMB, C2)) / np.sqrt(C2) / s[None, :]),
            'bn_g': bf(1.0 + 0.1 * np.random.standard_normal(EMB)),
            'bn_b': bf(0.3 * np.random.standard_normal(EMB))}


def reference(T1, T2, Wf, bn_g, bn_b):
    joint = np.concatenate([f64(T1).swapaxes(1, 2), f64(T2).swapaxes(1, 2)], axis=1)
    y = mxq(f64(Wf), 1, 'e4m3') @ mxq(joint, 1, 'e4m3')
    mu = y.mean(axis=(0, 2), keepdims=True)
    var = y.var(axis=(0, 2), keepdims=True)
    y = (y - mu) / np.sqrt(var + BN_EPS)
    y = y * f64(bn_g)[None, :, None] + f64(bn_b)[None, :, None]
    y = np.maximum(y, 0.0)
    return y.swapaxes(1, 2)

@@ -1,0 +1,199 @@
+from contextlib import ExitStack
+
+import concourse.mybir as mybir
+from concourse.masks import make_identity
+
+F32 = mybir.dt.float32
+BF16 = mybir.dt.bfloat16
+U32 = mybir.dt.uint32
+U8 = mybir.dt.uint8
+FP8X4 = mybir.dt.float8_e4m3fn_x4
+ACT = mybir.ActivationFunctionType
+ALU = mybir.AluOpType
+
+P = 128
+PACK = 4
+STREAMS = 2
+ROWS = 1024
+EMB = 256
+K = STREAMS * EMB
+WORDS = EMB // 2
+O_TILES = EMB // P
+ROW_TILES = ROWS // P
+CHUNKS = 2
+TILES_PER_CHUNK = ROW_TILES // CHUNKS
+CHUNK_ROWS = TILES_PER_CHUNK * P
+TILES_PER_BANK = 2
+BANKS_PER_CHUNK = TILES_PER_CHUNK // TILES_PER_BANK
+BN_EPS = 1e-5
+BN_STATS_DIM = 6
+
+FLOPS = 2 * ROWS * K * EMB
+
+
+def tile_iag_pb_s_kernel(tc, T1, T2, Wf, bn_g, bn_b, out):
+    nc = tc.nc
+    streams = [
+        T.flatten_outer_dims().rearrange("(p j) k -> p j k", j=ROW_TILES) for T in (T1, T2)
+    ]
+    out_rows = out.flatten_outer_dims().rearrange("(p j) o -> p j o", j=ROW_TILES)
+
+    with ExitStack() as ctx:
+        keep = ctx.enter_context(tc.tile_pool(name="keep", bufs=1))
+        flip = ctx.enter_context(tc.psum_pool(name="flip", bufs=4))
+        prod = ctx.enter_context(tc.psum_pool(name="prod", bufs=O_TILES * CHUNKS))
+
+        w_raw = keep.tile([P, O_TILES * K], BF16)
+        nc.sync.dma_start(
+            out=w_raw[:].rearrange("p (t k) -> p t k", t=O_TILES),
+            in_=Wf.rearrange("(t p) k -> p t k", p=P),
+        )
+        x_raw = []
+        for c in range(CHUNKS):
+            raw = keep.tile([P, STREAMS * TILES_PER_CHUNK * EMB], BF16, name="x_raw%d" % c)
+            x_raw.append(raw)
+            for u in range(STREAMS):
+                nc.sync.dma_start(
+                    out=raw[:].rearrange("p (u j k) -> p u j k", u=STREAMS, j=TILES_PER_CHUNK)[
+                        :, u, :, :
+                    ],
+                    in_=streams[u][:, c * TILES_PER_CHUNK : (c + 1) * TILES_PER_CHUNK, :],
+                )
+
+        ident = keep.tile([P, P], F32)
+        make_identity(nc, ident[:])
+        eps = keep.tile([P, 1], F32)
+        nc.vector.memset(eps[:], BN_EPS)
+        table_warm = keep.tile([P, 1], F32)
+        nc.scalar.activation(out=table_warm[:], in_=eps[:], func=ACT.Sqrt)
+
+        gb_rows = keep.tile([P, P], BF16)
+        nc.vector.memset(gb_rows[:], 0.0)
+        nc.scalar.dma_start(out=gb_rows[0:O_TILES, :], in_=bn_g.rearrange("(t o) -> t o", o=P))
+        nc.scalar.dma_start(
+            out=gb_rows[O_TILES : 2 * O_TILES, :], in_=bn_b.rearrange("(t o) -> t o", o=P)
+        )
+        gb_wide = keep.tile([P, P], F32)
+        nc.vector.tensor_copy(out=gb_wide[:], in_=gb_rows[:])
+
+        w_words = w_raw[:].bitcast(F32).rearrange("p (t u w) -> p t u w", t=O_TILES, u=STREAMS)
+        w_bank = flip.tile([P, O_TILES, STREAMS, P], F32, tag="bank")
+        for t in range(O_TILES):
+            for u in range(STREAMS):
+                nc.tensor.transpose(w_bank[:, t, u, :], w_words[:, t, u, :], ident[:])
+        w_grouped = keep.tile([P, EMB * PACK], BF16, align_bytes=64)
+        nc.scalar.copy(
+            out=w_grouped[:].bitcast(F32).rearrange("p (t o u) -> p t o u", t=O_TILES, u=STREAMS),
+            in_=w_bank[:].rearrange("p t u o -> p t o u"),
+        )
+        w_codes = keep.tile([P, EMB], U32, align_bytes=64)
+        w_scales = keep.tile([P, EMB], U8, align_bytes=64)
+        nc.vector.quantize_mx(
+            out=w_codes[:].bitcast(FP8X4), scales=w_scales[:], in_=w_grouped[:]
+        )
+
+        gb_bank = flip.tile([P, P], F32, tag="bank")
+        nc.tensor.transpose(gb_bank[:], gb_wide[:], ident[:])
+        gain_shift = keep.tile([P, 2 * O_TILES], F32)
+        nc.vector.tensor_copy(out=gain_shift[:], in_=gb_bank[:, 0 : 2 * O_TILES])
+        gain = gain_shift[:, 0:O_TILES]
+        shift_in = gain_shift[:, O_TILES : 2 * O_TILES]
+
+        stats = keep.tile([P, O_TILES, CHUNKS, BN_STATS_DIM], F32)
+        y = {}
+        for c in range(CHUNKS):
+            x_words = x_raw[c][:].bitcast(F32).rearrange(
+                "p (u j w) -> p u j w", u=STREAMS, j=TILES_PER_CHUNK
+            )
+            x_grouped = keep.tile([P, CHUNK_ROWS * PACK], BF16, align_bytes=64, name="x_grouped%d" % c)
+            x_grouped_words = x_grouped[:].bitcast(F32).rearrange(
+                "p (j r u) -> p j r u", j=TILES_PER_CHUNK, u=STREAMS
+            )
+            for h in range(BANKS_PER_CHUNK):
+                x_bank = flip.tile([P, TILES_PER_BANK, STREAMS, P], F32, tag="bank")
+                for i in range(TILES_PER_BANK):
+                    for u in range(STREAMS):
+                        nc.tensor.transpose(
+                            x_bank[:, i, u, :], x_words[:, u, h * TILES_PER_BANK + i, :], ident[:]
+                        )
+                copy_out = nc.scalar.copy if h % 2 == 0 else nc.vector.tensor_copy
+                copy_out(
+                    out=x_grouped_words[:, h * TILES_PER_BANK : (h + 1) * TILES_PER_BANK, :, :],
+                    in_=x_bank[:].rearrange("p i u r -> p i r u"),
+                )
+            x_codes = keep.tile([P, CHUNK_ROWS], U32, align_bytes=64, name="x_codes%d" % c)
+            x_scales = keep.tile([P, CHUNK_ROWS], U8, align_bytes=64, name="x_scales%d" % c)
+            nc.vector.quantize_mx(
+                out=x_codes[:].bitcast(FP8X4), scales=x_scales[:], in_=x_grouped[:]
+            )
+            for t in range(O_TILES):
+                o_cols = slice(t * P, (t + 1) * P)
+                y[t, c] = prod.tile([P, CHUNK_ROWS], F32, tag="y", name="y%d%d" % (t, c))
+                nc.tensor.matmul_mx(
+                    out=y[t, c][:],
+                    lhsT=w_codes[:, o_cols].bitcast(FP8X4),
+                    lhsT_scale=w_scales[:, o_cols],
+                    rhs=x_codes[:].bitcast(FP8X4),
+                    rhs_scale=x_scales[:],
+                    start=True,
+                    stop=True,
+                )
+                nc.vector.bn_stats(out=stats[:, t, c, :], in_=y[t, c][:])
+
+        mean_var = keep.tile([P, O_TILES, 2], F32)
+        for t in range(O_TILES):
+            nc.vector.bn_aggr(
+                out=mean_var[:, t, :], in_=stats[:, t, :, :].rearrange("p c s -> p (c s)")
+            )
+        std = keep.tile([P, O_TILES], F32)
+        nc.scalar.activation(out=std[:], in_=mean_var[:, :, 1], func=ACT.Sqrt, bias=eps[:, 0:1])
+        rstd = keep.tile([P, O_TILES], F32)
+        nc.vector.reciprocal(out=rstd[:], in_=std[:])
+        scale = keep.tile([P, O_TILES], F32)
+        nc.vector.tensor_mul(out=scale[:], in0=rstd[:], in1=gain)
+        mean_scaled = keep.tile([P, O_TILES], F32)
+        nc.vector.tensor_mul(out=mean_scaled[:], in0=mean_var[:, :, 0], in1=scale[:])
+        shift = keep.tile([P, O_TILES], F32)
+        nc.vector.tensor_sub(out=shift[:], in0=shift_in, in1=mean_scaled[:])
+
+        for c in range(CHUNKS):
+            z = []
+            for t in range(O_TILES):
+                z_t = keep.tile([P, CHUNK_ROWS], F32, name="z%d%d" % (t, c))
+                z.append(z_t)
+                if t == 0:
+                    nc.scalar.activation(
+                        out=z_t[:],
+                        in_=y[t, c][:],
+                        func=ACT.Identity,
+                        scale=scale[:, t : t + 1],
+                        bias=shift[:, t : t + 1],
+                    )
+                else:
+                    nc.vector.tensor_scalar(
+                        out=z_t[:],
+                        in0=y[t, c][:],
+                        scalar1=scale[:, t : t + 1],
+                        scalar2=shift[:, t : t + 1],
+                        op0=ALU.mult,
+                        op1=ALU.add,
+                    )
+            result = keep.tile([P, TILES_PER_CHUNK, EMB], F32, name="result%d" % c)
+            for h in range(BANKS_PER_CHUNK):
+                out_bank = flip.tile([P, TILES_PER_BANK, EMB], F32, tag="bank")
+                for i in range(TILES_PER_BANK):
+                    j = h * TILES_PER_BANK + i
+                    for t in range(O_TILES):
+                        nc.tensor.transpose(
+                            out_bank[:, i, t * P : (t + 1) * P],
+                            z[t][:, j * P : (j + 1) * P],
+                            ident[:],
+                        )
+                tiles = slice(h * TILES_PER_BANK, (h + 1) * TILES_PER_BANK)
+                if h % 2 == 0:
+                    nc.scalar.activation(out=result[:, tiles, :], in_=out_bank[:], func=ACT.Relu)
+                else:
+                    nc.vector.tensor_scalar_max(out=result[:, tiles, :], in0=out_bank[:], scalar1=0.0)
+            nc.sync.dma_start(
+                out=out_rows[:, c * TILES_PER_CHUNK : (c + 1) * TILES_PER_CHUNK, :], in_=result[:]
+            )

@@ -17,14 +17,15 @@ STREAMS = 2
 ROWS = 1024
 EMB = 256
 K = STREAMS * EMB
-WORDS = EMB // 2
 O_TILES = EMB // P
 ROW_TILES = ROWS // P
+UNIT_TILES = 2
+UNITS = ROW_TILES // UNIT_TILES
+UNIT_ROWS = UNIT_TILES * P
 CHUNKS = 2
-TILES_PER_CHUNK = ROW_TILES // CHUNKS
-CHUNK_ROWS = TILES_PER_CHUNK * P
-TILES_PER_BANK = 2
-BANKS_PER_CHUNK = TILES_PER_CHUNK // TILES_PER_BANK
+CHUNK_UNITS = UNITS // CHUNKS
+CHUNK_TILES = ROW_TILES // CHUNKS
+PSUM_BANKS = 8
 BN_EPS = 1e-5
 BN_STATS_DIM = 6
 
@@ -39,9 +40,9 @@ def tile_iag_pb_s_kernel(tc, T1, T2, Wf, bn_g, bn_b, out):
     out_rows = out.flatten_outer_dims().rearrange("(p j) o -> p j o", j=ROW_TILES)
 
     with ExitStack() as ctx:
+        ctx.enter_context(tc.manual_schedule())
         keep = ctx.enter_context(tc.tile_pool(name="keep", bufs=1))
-        flip = ctx.enter_context(tc.psum_pool(name="flip", bufs=4))
-        prod = ctx.enter_context(tc.psum_pool(name="prod", bufs=O_TILES * CHUNKS))
+        banks = ctx.enter_context(tc.psum_pool(name="banks", bufs=PSUM_BANKS))
 
         w_raw = keep.tile([P, O_TILES * K], BF16)
         nc.sync.dma_start(
@@ -50,15 +51,21 @@ def tile_iag_pb_s_kernel(tc, T1, T2, Wf, bn_g, bn_b, out):
         )
         x_raw = []
         for c in range(CHUNKS):
-            raw = keep.tile([P, STREAMS * TILES_PER_CHUNK * EMB], BF16, name="x_raw%d" % c)
+            raw = keep.tile([P, STREAMS * CHUNK_TILES * EMB], BF16, name="x_raw%d" % c)
             x_raw.append(raw)
             for u in range(STREAMS):
                 nc.sync.dma_start(
-                    out=raw[:].rearrange("p (u j k) -> p u j k", u=STREAMS, j=TILES_PER_CHUNK)[
+                    out=raw[:].rearrange("p (u j k) -> p u j k", u=STREAMS, j=CHUNK_TILES)[
                         :, u, :, :
                     ],
-                    in_=streams[u][:, c * TILES_PER_CHUNK : (c + 1) * TILES_PER_CHUNK, :],
+                    in_=streams[u][:, c * CHUNK_TILES : (c + 1) * CHUNK_TILES, :],
                 )
+        gb_rows = keep.tile([P, P], BF16)
+        nc.vector.memset(gb_rows[:], 0.0)
+        nc.scalar.dma_start(out=gb_rows[0:O_TILES, :], in_=bn_g.rearrange("(t o) -> t o", o=P))
+        nc.scalar.dma_start(
+            out=gb_rows[O_TILES : 2 * O_TILES, :], in_=bn_b.rearrange("(t o) -> t o", o=P)
+        )
 
         ident = keep.tile([P, P], F32)
         make_identity(nc, ident[:])
@@ -67,17 +74,8 @@ def tile_iag_pb_s_kernel(tc, T1, T2, Wf, bn_g, bn_b, out):
         table_warm = keep.tile([P, 1], F32)
         nc.scalar.activation(out=table_warm[:], in_=eps[:], func=ACT.Sqrt)
 
-        gb_rows = keep.tile([P, P], BF16)
-        nc.vector.memset(gb_rows[:], 0.0)
-        nc.scalar.dma_start(out=gb_rows[0:O_TILES, :], in_=bn_g.rearrange("(t o) -> t o", o=P))
-        nc.scalar.dma_start(
-            out=gb_rows[O_TILES : 2 * O_TILES, :], in_=bn_b.rearrange("(t o) -> t o", o=P)
-        )
-        gb_wide = keep.tile([P, P], F32)
-        nc.vector.tensor_copy(out=gb_wide[:], in_=gb_rows[:])
-
         w_words = w_raw[:].bitcast(F32).rearrange("p (t u w) -> p t u w", t=O_TILES, u=STREAMS)
-        w_bank = flip.tile([P, O_TILES, STREAMS, P], F32, tag="bank")
+        w_bank = banks.tile([P, O_TILES, STREAMS, P], F32, tag="bank")
         for t in range(O_TILES):
             for u in range(STREAMS):
                 nc.tensor.transpose(w_bank[:, t, u, :], w_words[:, t, u, :], ident[:])
@@ -92,108 +90,142 @@ def tile_iag_pb_s_kernel(tc, T1, T2, Wf, bn_g, bn_b, out):
             out=w_codes[:].bitcast(FP8X4), scales=w_scales[:], in_=w_grouped[:]
         )
 
-        gb_bank = flip.tile([P, P], F32, tag="bank")
+        x_banks = {}
+        x_codes = {}
+        x_scales = {}
+
+        def transpose_rows(c):
+            x_words = x_raw[c][:].bitcast(F32).rearrange(
+                "p (u n i w) -> p u n i w", u=STREAMS, n=CHUNK_UNITS, i=UNIT_TILES
+            )
+            for n in range(CHUNK_UNITS):
+                x_banks[c, n] = banks.tile(
+                    [P, UNIT_TILES, STREAMS, P], F32, tag="bank", name="x_bank%d%d" % (c, n)
+                )
+            for u in range(STREAMS):
+                for n in range(CHUNK_UNITS):
+                    for i in range(UNIT_TILES):
+                        nc.tensor.transpose(
+                            x_banks[c, n][:, i, u, :], x_words[:, u, n, i, :], ident[:]
+                        )
+
+        def group_and_quantise(c):
+            for n in range(CHUNK_UNITS):
+                unit = c * CHUNK_UNITS + n
+                x_grouped = keep.tile(
+                    [P, UNIT_ROWS * PACK], BF16, align_bytes=64, name="x_grouped%d" % unit
+                )
+                nc.scalar.copy(
+                    out=x_grouped[:].bitcast(F32).rearrange(
+                        "p (i r u) -> p i r u", i=UNIT_TILES, u=STREAMS
+                    ),
+                    in_=x_banks[c, n][:].rearrange("p i u r -> p i r u"),
+                )
+                x_codes[unit] = keep.tile(
+                    [P, UNIT_ROWS], U32, align_bytes=64, name="x_codes%d" % unit
+                )
+                x_scales[unit] = keep.tile(
+                    [P, UNIT_ROWS], U8, align_bytes=64, name="x_scales%d" % unit
+                )
+                nc.vector.quantize_mx(
+                    out=x_codes[unit][:].bitcast(FP8X4), scales=x_scales[unit][:], in_=x_grouped[:]
+                )
+
+        gb_wide = keep.tile([P, P], F32)
+        nc.vector.tensor_copy(out=gb_wide[:], in_=gb_rows[:])
+        transpose_rows(0)
+        gb_bank = banks.tile([P, P], F32, tag="bank")
         nc.tensor.transpose(gb_bank[:], gb_wide[:], ident[:])
+        group_and_quantise(0)
         gain_shift = keep.tile([P, 2 * O_TILES], F32)
         nc.vector.tensor_copy(out=gain_shift[:], in_=gb_bank[:, 0 : 2 * O_TILES])
         gain = gain_shift[:, 0:O_TILES]
         shift_in = gain_shift[:, O_TILES : 2 * O_TILES]
+        neg_gain = keep.tile([P, O_TILES], F32)
+        nc.vector.tensor_scalar_mul(out=neg_gain[:], in0=gain, scalar1=-1.0)
+        transpose_rows(1)
+        group_and_quantise(1)
 
-        stats = keep.tile([P, O_TILES, CHUNKS, BN_STATS_DIM], F32)
+        stats = keep.tile([P, O_TILES, UNITS, BN_STATS_DIM], F32)
         y = {}
-        for c in range(CHUNKS):
-            x_words = x_raw[c][:].bitcast(F32).rearrange(
-                "p (u j w) -> p u j w", u=STREAMS, j=TILES_PER_CHUNK
-            )
-            x_grouped = keep.tile([P, CHUNK_ROWS * PACK], BF16, align_bytes=64, name="x_grouped%d" % c)
-            x_grouped_words = x_grouped[:].bitcast(F32).rearrange(
-                "p (j r u) -> p j r u", j=TILES_PER_CHUNK, u=STREAMS
-            )
-            for h in range(BANKS_PER_CHUNK):
-                x_bank = flip.tile([P, TILES_PER_BANK, STREAMS, P], F32, tag="bank")
-                for i in range(TILES_PER_BANK):
-                    for u in range(STREAMS):
-                        nc.tensor.transpose(
-                            x_bank[:, i, u, :], x_words[:, u, h * TILES_PER_BANK + i, :], ident[:]
-                        )
-                copy_out = nc.scalar.copy if h % 2 == 0 else nc.vector.tensor_copy
-                copy_out(
-                    out=x_grouped_words[:, h * TILES_PER_BANK : (h + 1) * TILES_PER_BANK, :, :],
-                    in_=x_bank[:].rearrange("p i u r -> p i r u"),
-                )
-            x_codes = keep.tile([P, CHUNK_ROWS], U32, align_bytes=64, name="x_codes%d" % c)
-            x_scales = keep.tile([P, CHUNK_ROWS], U8, align_bytes=64, name="x_scales%d" % c)
-            nc.vector.quantize_mx(
-                out=x_codes[:].bitcast(FP8X4), scales=x_scales[:], in_=x_grouped[:]
-            )
+        for unit in range(UNITS):
             for t in range(O_TILES):
                 o_cols = slice(t * P, (t + 1) * P)
-                y[t, c] = prod.tile([P, CHUNK_ROWS], F32, tag="y", name="y%d%d" % (t, c))
+                y[t, unit] = banks.tile([P, UNIT_ROWS], F32, tag="bank", name="y%d%d" % (t, unit))
                 nc.tensor.matmul_mx(
-                    out=y[t, c][:],
+                    out=y[t, unit][:],
                     lhsT=w_codes[:, o_cols].bitcast(FP8X4),
                     lhsT_scale=w_scales[:, o_cols],
-                    rhs=x_codes[:].bitcast(FP8X4),
-                    rhs_scale=x_scales[:],
+                    rhs=x_codes[unit][:].bitcast(FP8X4),
+                    rhs_scale=x_scales[unit][:],
                     start=True,
                     stop=True,
                 )
-                nc.vector.bn_stats(out=stats[:, t, c, :], in_=y[t, c][:])
+                nc.vector.bn_stats(out=stats[:, t, unit, :], in_=y[t, unit][:])
 
         mean_var = keep.tile([P, O_TILES, 2], F32)
         for t in range(O_TILES):
             nc.vector.bn_aggr(
-                out=mean_var[:, t, :], in_=stats[:, t, :, :].rearrange("p c s -> p (c s)")
+                out=mean_var[:, t, :], in_=stats[:, t, :, :].rearrange("p n s -> p (n s)")
             )
         std = keep.tile([P, O_TILES], F32)
         nc.scalar.activation(out=std[:], in_=mean_var[:, :, 1], func=ACT.Sqrt, bias=eps[:, 0:1])
+        neg_mean_gain = keep.tile([P, O_TILES], F32)
+        nc.vector.tensor_mul(out=neg_mean_gain[:], in0=mean_var[:, :, 0], in1=neg_gain[:])
         rstd = keep.tile([P, O_TILES], F32)
         nc.vector.reciprocal(out=rstd[:], in_=std[:])
         scale = keep.tile([P, O_TILES], F32)
         nc.vector.tensor_mul(out=scale[:], in0=rstd[:], in1=gain)
-        mean_scaled = keep.tile([P, O_TILES], F32)
-        nc.vector.tensor_mul(out=mean_scaled[:], in0=mean_var[:, :, 0], in1=scale[:])
         shift = keep.tile([P, O_TILES], F32)
-        nc.vector.tensor_sub(out=shift[:], in0=shift_in, in1=mean_scaled[:])
-
-        for c in range(CHUNKS):
-            z = []
-            for t in range(O_TILES):
-                z_t = keep.tile([P, CHUNK_ROWS], F32, name="z%d%d" % (t, c))
-                z.append(z_t)
-                if t == 0:
-                    nc.scalar.activation(
-                        out=z_t[:],
-                        in_=y[t, c][:],
-                        func=ACT.Identity,
-                        scale=scale[:, t : t + 1],
-                        bias=shift[:, t : t + 1],
-                    )
-                else:
-                    nc.vector.tensor_scalar(
-                        out=z_t[:],
-                        in0=y[t, c][:],
-                        scalar1=scale[:, t : t + 1],
-                        scalar2=shift[:, t : t + 1],
-                        op0=ALU.mult,
-                        op1=ALU.add,
-                    )
-            result = keep.tile([P, TILES_PER_CHUNK, EMB], F32, name="result%d" % c)
-            for h in range(BANKS_PER_CHUNK):
-                out_bank = flip.tile([P, TILES_PER_BANK, EMB], F32, tag="bank")
-                for i in range(TILES_PER_BANK):
-                    j = h * TILES_PER_BANK + i
-                    for t in range(O_TILES):
-                        nc.tensor.transpose(
-                            out_bank[:, i, t * P : (t + 1) * P],
-                            z[t][:, j * P : (j + 1) * P],
-                            ident[:],
-                        )
-                tiles = slice(h * TILES_PER_BANK, (h + 1) * TILES_PER_BANK)
-                if h % 2 == 0:
-                    nc.scalar.activation(out=result[:, tiles, :], in_=out_bank[:], func=ACT.Relu)
-                else:
-                    nc.vector.tensor_scalar_max(out=result[:, tiles, :], in0=out_bank[:], scalar1=0.0)
-            nc.sync.dma_start(
-                out=out_rows[:, c * TILES_PER_CHUNK : (c + 1) * TILES_PER_CHUNK, :], in_=result[:]
+        for t in range(O_TILES):
+            nc.vector.tensor_scalar(
+                out=shift[:, t : t + 1],
+                in0=neg_mean_gain[:, t : t + 1],
+                scalar1=rstd[:, t : t + 1],
+                scalar2=shift_in[:, t : t + 1],
+                op0=ALU.mult,
+                op1=ALU.add,
             )
+
+        z = {}
+
+        def normalise(unit):
+            for t in range(O_TILES):
+                z[t, unit] = keep.tile([P, UNIT_ROWS], F32, name="z%d%d" % (t, unit))
+            nc.scalar.activation(
+                out=z[0, unit][:],
+                in_=y[0, unit][:],
+                func=ACT.Identity,
+                scale=scale[:, 0:1],
+                bias=shift[:, 0:1],
+            )
+            nc.vector.tensor_scalar(
+                out=z[1, unit][:],
+                in0=y[1, unit][:],
+                scalar1=scale[:, 1:2],
+                scalar2=shift[:, 1:2],
+                op0=ALU.mult,
+                op1=ALU.add,
+            )
+
+        def finish(unit):
+            result = keep.tile([P, UNIT_TILES, EMB], F32, name="result%d" % unit)
+            for i in range(UNIT_TILES):
+                out_bank = banks.tile([P, EMB], F32, tag="bank", name="out_bank%d%d" % (unit, i))
+                for t in range(O_TILES):
+                    nc.tensor.transpose(
+                        out_bank[:, t * P : (t + 1) * P], z[t, unit][:, i * P : (i + 1) * P], ident[:]
+                    )
+                if i == 0:
+                    nc.scalar.activation(out=result[:, i, :], in_=out_bank[:], func=ACT.Relu)
+                else:
+                    nc.vector.tensor_scalar_max(out=result[:, i, :], in0=out_bank[:], scalar1=0.0)
+            nc.sync.dma_start(
+                out=out_rows[:, unit * UNIT_TILES : (unit + 1) * UNIT_TILES, :], in_=result[:]
+            )
+
+        normalise(0)
+        for unit in range(UNITS):
+            if unit + 1 < UNITS:
+                normalise(unit + 1)
+            finish(unit)

@@ -26,6 +26,7 @@ CHUNKS = 2
 CHUNK_UNITS = UNITS // CHUNKS
 CHUNK_TILES = ROW_TILES // CHUNKS
 PSUM_BANKS = 8
+LEAD = 2
 BN_EPS = 1e-5
 BN_STATS_DIM = 6
 
@@ -72,7 +73,7 @@ def tile_iag_pb_s_kernel(tc, T1, T2, Wf, bn_g, bn_b, out):
         eps = keep.tile([P, 1], F32)
         nc.vector.memset(eps[:], BN_EPS)
         table_warm = keep.tile([P, 1], F32)
-        nc.scalar.activation(out=table_warm[:], in_=eps[:], func=ACT.Sqrt)
+        nc.scalar.activation(out=table_warm[:], in_=eps[:], func=ACT.Abs_reciprocal_sqrt)
 
         w_words = w_raw[:].bitcast(F32).rearrange("p (t u w) -> p t u w", t=O_TILES, u=STREAMS)
         w_bank = banks.tile([P, O_TILES, STREAMS, P], F32, tag="bank")
@@ -99,56 +100,42 @@ def tile_iag_pb_s_kernel(tc, T1, T2, Wf, bn_g, bn_b, out):
                 "p (u n i w) -> p u n i w", u=STREAMS, n=CHUNK_UNITS, i=UNIT_TILES
             )
             for n in range(CHUNK_UNITS):
-                x_banks[c, n] = banks.tile(
+                x_banks[c * CHUNK_UNITS + n] = banks.tile(
                     [P, UNIT_TILES, STREAMS, P], F32, tag="bank", name="x_bank%d%d" % (c, n)
                 )
             for u in range(STREAMS):
                 for n in range(CHUNK_UNITS):
                     for i in range(UNIT_TILES):
                         nc.tensor.transpose(
-                            x_banks[c, n][:, i, u, :], x_words[:, u, n, i, :], ident[:]
+                            x_banks[c * CHUNK_UNITS + n][:, i, u, :], x_words[:, u, n, i, :], ident[:]
                         )
 
-        def group_and_quantise(c):
-            for n in range(CHUNK_UNITS):
-                unit = c * CHUNK_UNITS + n
-                x_grouped = keep.tile(
-                    [P, UNIT_ROWS * PACK], BF16, align_bytes=64, name="x_grouped%d" % unit
-                )
-                nc.scalar.copy(
-                    out=x_grouped[:].bitcast(F32).rearrange(
-                        "p (i r u) -> p i r u", i=UNIT_TILES, u=STREAMS
-                    ),
-                    in_=x_banks[c, n][:].rearrange("p i u r -> p i r u"),
-                )
-                x_codes[unit] = keep.tile(
-                    [P, UNIT_ROWS], U32, align_bytes=64, name="x_codes%d" % unit
-                )
-                x_scales[unit] = keep.tile(
-                    [P, UNIT_ROWS], U8, align_bytes=64, name="x_scales%d" % unit
-                )
-                nc.vector.quantize_mx(
-                    out=x_codes[unit][:].bitcast(FP8X4), scales=x_scales[unit][:], in_=x_grouped[:]
-                )
+        x_grouped = {}
 
-        gb_wide = keep.tile([P, P], F32)
-        nc.vector.tensor_copy(out=gb_wide[:], in_=gb_rows[:])
-        transpose_rows(0)
-        gb_bank = banks.tile([P, P], F32, tag="bank")
-        nc.tensor.transpose(gb_bank[:], gb_wide[:], ident[:])
-        group_and_quantise(0)
-        gain_shift = keep.tile([P, 2 * O_TILES], F32)
-        nc.vector.tensor_copy(out=gain_shift[:], in_=gb_bank[:, 0 : 2 * O_TILES])
-        gain = gain_shift[:, 0:O_TILES]
-        shift_in = gain_shift[:, O_TILES : 2 * O_TILES]
-        neg_gain = keep.tile([P, O_TILES], F32)
-        nc.vector.tensor_scalar_mul(out=neg_gain[:], in0=gain, scalar1=-1.0)
-        transpose_rows(1)
-        group_and_quantise(1)
+        def group(unit):
+            x_grouped[unit] = keep.tile(
+                [P, UNIT_ROWS * PACK], BF16, align_bytes=64, name="x_grouped%d" % unit
+            )
+            nc.scalar.copy(
+                out=x_grouped[unit][:].bitcast(F32).rearrange(
+                    "p (i r u) -> p i r u", i=UNIT_TILES, u=STREAMS
+                ),
+                in_=x_banks[unit][:].rearrange("p i u r -> p i r u"),
+            )
+
+        def quantise(unit):
+            x_codes[unit] = keep.tile([P, UNIT_ROWS], U32, align_bytes=64, name="x_codes%d" % unit)
+            x_scales[unit] = keep.tile([P, UNIT_ROWS], U8, align_bytes=64, name="x_scales%d" % unit)
+            nc.vector.quantize_mx(
+                out=x_codes[unit][:].bitcast(FP8X4),
+                scales=x_scales[unit][:],
+                in_=x_grouped[unit][:],
+            )
 
         stats = keep.tile([P, O_TILES, UNITS, BN_STATS_DIM], F32)
         y = {}
-        for unit in range(UNITS):
+
+        def multiply(unit):
             for t in range(O_TILES):
                 o_cols = slice(t * P, (t + 1) * P)
                 y[t, unit] = banks.tile([P, UNIT_ROWS], F32, tag="bank", name="y%d%d" % (t, unit))
@@ -161,19 +148,48 @@ def tile_iag_pb_s_kernel(tc, T1, T2, Wf, bn_g, bn_b, out):
                     start=True,
                     stop=True,
                 )
+
+        def sum_up(unit):
+            for t in range(O_TILES):
                 nc.vector.bn_stats(out=stats[:, t, unit, :], in_=y[t, unit][:])
+
+        gb_wide = keep.tile([P, P], F32)
+        nc.vector.tensor_copy(out=gb_wide[:], in_=gb_rows[:])
+        transpose_rows(0)
+        gb_bank = banks.tile([P, P], F32, tag="bank")
+        nc.tensor.transpose(gb_bank[:], gb_wide[:], ident[:])
+        for unit in range(CHUNK_UNITS):
+            group(unit)
+            quantise(unit)
+        gain_shift = keep.tile([P, 2 * O_TILES], F32)
+        nc.vector.tensor_copy(out=gain_shift[:], in_=gb_bank[:, 0 : 2 * O_TILES])
+        gain = gain_shift[:, 0:O_TILES]
+        shift_in = gain_shift[:, O_TILES : 2 * O_TILES]
+        neg_gain = keep.tile([P, O_TILES], F32)
+        nc.vector.tensor_scalar_mul(out=neg_gain[:], in0=gain, scalar1=-1.0)
+
+        transpose_rows(1)
+        for unit in range(CHUNK_UNITS):
+            multiply(unit)
+        for unit in range(CHUNK_UNITS):
+            group(CHUNK_UNITS + unit)
+            sum_up(unit)
+            quantise(CHUNK_UNITS + unit)
+        for unit in range(CHUNK_UNITS, UNITS):
+            multiply(unit)
+            sum_up(unit)
 
         mean_var = keep.tile([P, O_TILES, 2], F32)
         for t in range(O_TILES):
             nc.vector.bn_aggr(
                 out=mean_var[:, t, :], in_=stats[:, t, :, :].rearrange("p n s -> p (n s)")
             )
-        std = keep.tile([P, O_TILES], F32)
-        nc.scalar.activation(out=std[:], in_=mean_var[:, :, 1], func=ACT.Sqrt, bias=eps[:, 0:1])
+        rstd = keep.tile([P, O_TILES], F32)
+        nc.scalar.activation(
+            out=rstd[:], in_=mean_var[:, :, 1], func=ACT.Abs_reciprocal_sqrt, bias=eps[:, 0:1]
+        )
         neg_mean_gain = keep.tile([P, O_TILES], F32)
         nc.vector.tensor_mul(out=neg_mean_gain[:], in0=mean_var[:, :, 0], in1=neg_gain[:])
-        rstd = keep.tile([P, O_TILES], F32)
-        nc.vector.reciprocal(out=rstd[:], in_=std[:])
         scale = keep.tile([P, O_TILES], F32)
         nc.vector.tensor_mul(out=scale[:], in0=rstd[:], in1=gain)
         shift = keep.tile([P, O_TILES], F32)
@@ -220,12 +236,11 @@ def tile_iag_pb_s_kernel(tc, T1, T2, Wf, bn_g, bn_b, out):
                     nc.scalar.activation(out=result[:, i, :], in_=out_bank[:], func=ACT.Relu)
                 else:
                     nc.vector.tensor_scalar_max(out=result[:, i, :], in0=out_bank[:], scalar1=0.0)
-            nc.sync.dma_start(
-                out=out_rows[:, unit * UNIT_TILES : (unit + 1) * UNIT_TILES, :], in_=result[:]
-            )
+                nc.sync.dma_start(out=out_rows[:, unit * UNIT_TILES + i, :], in_=result[:, i, :])
 
-        normalise(0)
+        for unit in range(LEAD):
+            normalise(unit)
         for unit in range(UNITS):
-            if unit + 1 < UNITS:
-                normalise(unit + 1)
+            if unit + LEAD < UNITS:
+                normalise(unit + LEAD)
             finish(unit)

@@ -26,7 +26,6 @@ CHUNKS = 2
 CHUNK_UNITS = UNITS // CHUNKS
 CHUNK_TILES = ROW_TILES // CHUNKS
 PSUM_BANKS = 8
-LEAD = 2
 BN_EPS = 1e-5
 BN_STATS_DIM = 6
 
@@ -208,21 +207,14 @@ def tile_iag_pb_s_kernel(tc, T1, T2, Wf, bn_g, bn_b, out):
         def normalise(unit):
             for t in range(O_TILES):
                 z[t, unit] = keep.tile([P, UNIT_ROWS], F32, name="z%d%d" % (t, unit))
-            nc.scalar.activation(
-                out=z[0, unit][:],
-                in_=y[0, unit][:],
-                func=ACT.Identity,
-                scale=scale[:, 0:1],
-                bias=shift[:, 0:1],
-            )
-            nc.vector.tensor_scalar(
-                out=z[1, unit][:],
-                in0=y[1, unit][:],
-                scalar1=scale[:, 1:2],
-                scalar2=shift[:, 1:2],
-                op0=ALU.mult,
-                op1=ALU.add,
-            )
+                nc.vector.tensor_scalar(
+                    out=z[t, unit][:],
+                    in0=y[t, unit][:],
+                    scalar1=scale[:, t : t + 1],
+                    scalar2=shift[:, t : t + 1],
+                    op0=ALU.mult,
+                    op1=ALU.add,
+                )
 
         def finish(unit):
             result = keep.tile([P, UNIT_TILES, EMB], F32, name="result%d" % unit)
@@ -232,15 +224,9 @@ def tile_iag_pb_s_kernel(tc, T1, T2, Wf, bn_g, bn_b, out):
                     nc.tensor.transpose(
                         out_bank[:, t * P : (t + 1) * P], z[t, unit][:, i * P : (i + 1) * P], ident[:]
                     )
-                if i == 0:
-                    nc.scalar.activation(out=result[:, i, :], in_=out_bank[:], func=ACT.Relu)
-                else:
-                    nc.vector.tensor_scalar_max(out=result[:, i, :], in0=out_bank[:], scalar1=0.0)
+                nc.scalar.activation(out=result[:, i, :], in_=out_bank[:], func=ACT.Relu)
                 nc.sync.dma_start(out=out_rows[:, unit * UNIT_TILES + i, :], in_=result[:, i, :])
 
-        for unit in range(LEAD):
-            normalise(unit)
         for unit in range(UNITS):
-            if unit + LEAD < UNITS:
-                normalise(unit + LEAD)
+            normalise(unit)
             finish(unit)

@@ -134,23 +134,91 @@ def tile_iag_pb_s_kernel(tc, T1, T2, Wf, bn_g, bn_b, out):
         stats = keep.tile([P, O_TILES, UNITS, BN_STATS_DIM], F32)
         y = {}
 
-        def multiply(unit):
-            for t in range(O_TILES):
-                o_cols = slice(t * P, (t + 1) * P)
-                y[t, unit] = banks.tile([P, UNIT_ROWS], F32, tag="bank", name="y%d%d" % (t, unit))
-                nc.tensor.matmul_mx(
-                    out=y[t, unit][:],
-                    lhsT=w_codes[:, o_cols].bitcast(FP8X4),
-                    lhsT_scale=w_scales[:, o_cols],
-                    rhs=x_codes[unit][:].bitcast(FP8X4),
-                    rhs_scale=x_scales[unit][:],
-                    start=True,
-                    stop=True,
+        def multiply(t, unit):
+            o_cols = slice(t * P, (t + 1) * P)
+            y[t, unit] = banks.tile([P, UNIT_ROWS], F32, tag="bank", name="y%d%d" % (t, unit))
+            nc.tensor.matmul_mx(
+                out=y[t, unit][:],
+                lhsT=w_codes[:, o_cols].bitcast(FP8X4),
+                lhsT_scale=w_scales[:, o_cols],
+                rhs=x_codes[unit][:].bitcast(FP8X4),
+                rhs_scale=x_scales[unit][:],
+                start=True,
+                stop=True,
+            )
+
+        def sum_up(t, unit):
+            nc.vector.bn_stats(out=stats[:, t, unit, :], in_=y[t, unit][:])
+
+        rstd = {}
+        neg_mean_gain = {}
+        scale = {}
+        shift = {}
+
+        def aggregate(t):
+            mean_var = keep.tile([P, 2], F32, name="mean_var%d" % t)
+            nc.vector.bn_aggr(out=mean_var[:], in_=stats[:, t, :, :].rearrange("p n s -> p (n s)"))
+            rstd[t] = keep.tile([P, 1], F32, name="rstd%d" % t)
+            nc.scalar.activation(
+                out=rstd[t][:], in_=mean_var[:, 1:2], func=ACT.Abs_reciprocal_sqrt, bias=eps[:, 0:1]
+            )
+            neg_mean_gain[t] = keep.tile([P, 1], F32, name="neg_mean_gain%d" % t)
+            nc.vector.tensor_mul(
+                out=neg_mean_gain[t][:], in0=mean_var[:, 0:1], in1=neg_gain[:, t : t + 1]
+            )
+
+        def scale_and_shift(t):
+            scale[t] = keep.tile([P, 1], F32, name="scale%d" % t)
+            nc.vector.tensor_mul(out=scale[t][:], in0=rstd[t][:], in1=gain[:, t : t + 1])
+            shift[t] = keep.tile([P, 1], F32, name="shift%d" % t)
+            nc.vector.tensor_scalar(
+                out=shift[t][:],
+                in0=neg_mean_gain[t][:],
+                scalar1=rstd[t][:],
+                scalar2=shift_in[:, t : t + 1],
+                op0=ALU.mult,
+                op1=ALU.add,
+            )
+
+        z = {}
+        out_banks = {}
+
+        def normalise(t, unit):
+            z[t, unit] = keep.tile([P, UNIT_ROWS], F32, name="z%d%d" % (t, unit))
+            if t == 0:
+                nc.scalar.activation(
+                    out=z[t, unit][:],
+                    in_=y[t, unit][:],
+                    func=ACT.Identity,
+                    scale=scale[t][:],
+                    bias=shift[t][:],
+                )
+            else:
+                nc.vector.tensor_scalar(
+                    out=z[t, unit][:],
+                    in0=y[t, unit][:],
+                    scalar1=scale[t][:],
+                    scalar2=shift[t][:],
+                    op0=ALU.mult,
+                    op1=ALU.add,
                 )
 
-        def sum_up(unit):
-            for t in range(O_TILES):
-                nc.vector.bn_stats(out=stats[:, t, unit, :], in_=y[t, unit][:])
+        def transpose_back(t, unit):
+            out_banks[t, unit] = banks.tile(
+                [P, UNIT_TILES, P], F32, tag="bank", name="out_bank%d%d" % (t, unit)
+            )
+            for i in range(UNIT_TILES):
+                nc.tensor.transpose(
+                    out_banks[t, unit][:, i, :], z[t, unit][:, i * P : (i + 1) * P], ident[:]
+                )
+
+        def relu_and_store(t, unit):
+            result = keep.tile([P, UNIT_TILES, P], F32, name="result%d%d" % (t, unit))
+            nc.scalar.activation(out=result[:], in_=out_banks[t, unit][:], func=ACT.Relu)
+            nc.sync.dma_start(
+                out=out_rows[:, unit * UNIT_TILES : (unit + 1) * UNIT_TILES, t * P : (t + 1) * P],
+                in_=result[:],
+            )
 
         gb_wide = keep.tile([P, P], F32)
         nc.vector.tensor_copy(out=gb_wide[:], in_=gb_rows[:])
@@ -168,65 +236,31 @@ def tile_iag_pb_s_kernel(tc, T1, T2, Wf, bn_g, bn_b, out):
         nc.vector.tensor_scalar_mul(out=neg_gain[:], in0=gain, scalar1=-1.0)
 
         transpose_rows(1)
+
         for unit in range(CHUNK_UNITS):
-            multiply(unit)
+            multiply(0, unit)
         for unit in range(CHUNK_UNITS):
             group(CHUNK_UNITS + unit)
-            sum_up(unit)
+            sum_up(0, unit)
             quantise(CHUNK_UNITS + unit)
         for unit in range(CHUNK_UNITS, UNITS):
-            multiply(unit)
-            sum_up(unit)
-
-        mean_var = keep.tile([P, O_TILES, 2], F32)
-        for t in range(O_TILES):
-            nc.vector.bn_aggr(
-                out=mean_var[:, t, :], in_=stats[:, t, :, :].rearrange("p n s -> p (n s)")
-            )
-        rstd = keep.tile([P, O_TILES], F32)
-        nc.scalar.activation(
-            out=rstd[:], in_=mean_var[:, :, 1], func=ACT.Abs_reciprocal_sqrt, bias=eps[:, 0:1]
-        )
-        neg_mean_gain = keep.tile([P, O_TILES], F32)
-        nc.vector.tensor_mul(out=neg_mean_gain[:], in0=mean_var[:, :, 0], in1=neg_gain[:])
-        scale = keep.tile([P, O_TILES], F32)
-        nc.vector.tensor_mul(out=scale[:], in0=rstd[:], in1=gain)
-        shift = keep.tile([P, O_TILES], F32)
-        for t in range(O_TILES):
-            nc.vector.tensor_scalar(
-                out=shift[:, t : t + 1],
-                in0=neg_mean_gain[:, t : t + 1],
-                scalar1=rstd[:, t : t + 1],
-                scalar2=shift_in[:, t : t + 1],
-                op0=ALU.mult,
-                op1=ALU.add,
-            )
-
-        z = {}
-
-        def normalise(unit):
-            for t in range(O_TILES):
-                z[t, unit] = keep.tile([P, UNIT_ROWS], F32, name="z%d%d" % (t, unit))
-                nc.vector.tensor_scalar(
-                    out=z[t, unit][:],
-                    in0=y[t, unit][:],
-                    scalar1=scale[:, t : t + 1],
-                    scalar2=shift[:, t : t + 1],
-                    op0=ALU.mult,
-                    op1=ALU.add,
-                )
-
-        def finish(unit):
-            result = keep.tile([P, UNIT_TILES, EMB], F32, name="result%d" % unit)
-            for i in range(UNIT_TILES):
-                out_bank = banks.tile([P, EMB], F32, tag="bank", name="out_bank%d%d" % (unit, i))
-                for t in range(O_TILES):
-                    nc.tensor.transpose(
-                        out_bank[:, t * P : (t + 1) * P], z[t, unit][:, i * P : (i + 1) * P], ident[:]
-                    )
-                nc.scalar.activation(out=result[:, i, :], in_=out_bank[:], func=ACT.Relu)
-                nc.sync.dma_start(out=out_rows[:, unit * UNIT_TILES + i, :], in_=result[:, i, :])
-
+            multiply(0, unit)
+            sum_up(0, unit)
         for unit in range(UNITS):
-            normalise(unit)
-            finish(unit)
+            multiply(1, unit)
+        aggregate(0)
+        sum_up(1, 0)
+        scale_and_shift(0)
+        for unit in range(UNITS):
+            normalise(0, unit)
+            transpose_back(0, unit)
+        for unit in range(1, UNITS):
+            sum_up(1, unit)
+        aggregate(1)
+        scale_and_shift(1)
+        for unit in range(UNITS):
+            relu_and_store(0, unit)
+        for unit in range(UNITS):
+            normalise(1, unit)
+            transpose_back(1, unit)
+            relu_and_store(1, unit)

from contextlib import ExitStack

import concourse.mybir as mybir
from concourse.masks import make_identity

F32 = mybir.dt.float32
BF16 = mybir.dt.bfloat16
U32 = mybir.dt.uint32
U8 = mybir.dt.uint8
FP8X4 = mybir.dt.float8_e4m3fn_x4
ACT = mybir.ActivationFunctionType
ALU = mybir.AluOpType

P = 128
PACK = 4
STREAMS = 2
ROWS = 1024
EMB = 256
K = STREAMS * EMB
O_TILES = EMB // P
ROW_TILES = ROWS // P
UNIT_TILES = 2
UNITS = ROW_TILES // UNIT_TILES
UNIT_ROWS = UNIT_TILES * P
CHUNKS = 2
CHUNK_UNITS = UNITS // CHUNKS
CHUNK_TILES = ROW_TILES // CHUNKS
PSUM_BANKS = 8
BN_EPS = 1e-5
BN_STATS_DIM = 6

FLOPS = 2 * ROWS * K * EMB


def tile_iag_pb_s_kernel(tc, T1, T2, Wf, bn_g, bn_b, out):
    nc = tc.nc
    streams = [
        T.flatten_outer_dims().rearrange("(p j) k -> p j k", j=ROW_TILES) for T in (T1, T2)
    ]
    out_rows = out.flatten_outer_dims().rearrange("(p j) o -> p j o", j=ROW_TILES)

    with ExitStack() as ctx:
        ctx.enter_context(tc.manual_schedule())
        keep = ctx.enter_context(tc.tile_pool(name="keep", bufs=1))
        banks = ctx.enter_context(tc.psum_pool(name="banks", bufs=PSUM_BANKS))

        w_raw = keep.tile([P, O_TILES * K], BF16)
        nc.sync.dma_start(
            out=w_raw[:].rearrange("p (t k) -> p t k", t=O_TILES),
            in_=Wf.rearrange("(t p) k -> p t k", p=P),
        )
        x_raw = []
        for c in range(CHUNKS):
            raw = keep.tile([P, STREAMS * CHUNK_TILES * EMB], BF16, name="x_raw%d" % c)
            x_raw.append(raw)
            for u in range(STREAMS):
                nc.sync.dma_start(
                    out=raw[:].rearrange("p (u j k) -> p u j k", u=STREAMS, j=CHUNK_TILES)[
                        :, u, :, :
                    ],
                    in_=streams[u][:, c * CHUNK_TILES : (c + 1) * CHUNK_TILES, :],
                )
        gb_rows = keep.tile([P, P], BF16)
        nc.vector.memset(gb_rows[:], 0.0)
        nc.scalar.dma_start(out=gb_rows[0:O_TILES, :], in_=bn_g.rearrange("(t o) -> t o", o=P))
        nc.scalar.dma_start(
            out=gb_rows[O_TILES : 2 * O_TILES, :], in_=bn_b.rearrange("(t o) -> t o", o=P)
        )

        ident = keep.tile([P, P], F32)
        make_identity(nc, ident[:])
        eps = keep.tile([P, 1], F32)
        nc.vector.memset(eps[:], BN_EPS)
        table_warm = keep.tile([P, 1], F32)
        nc.scalar.activation(out=table_warm[:], in_=eps[:], func=ACT.Abs_reciprocal_sqrt)

        w_words = w_raw[:].bitcast(F32).rearrange("p (t u w) -> p t u w", t=O_TILES, u=STREAMS)
        w_bank = banks.tile([P, O_TILES, STREAMS, P], F32, tag="bank")
        for t in range(O_TILES):
            for u in range(STREAMS):
                nc.tensor.transpose(w_bank[:, t, u, :], w_words[:, t, u, :], ident[:])
        w_grouped = keep.tile([P, EMB * PACK], BF16, align_bytes=64)
        nc.scalar.copy(
            out=w_grouped[:].bitcast(F32).rearrange("p (t o u) -> p t o u", t=O_TILES, u=STREAMS),
            in_=w_bank[:].rearrange("p t u o -> p t o u"),
        )
        w_codes = keep.tile([P, EMB], U32, align_bytes=64)
        w_scales = keep.tile([P, EMB], U8, align_bytes=64)
        nc.vector.quantize_mx(
            out=w_codes[:].bitcast(FP8X4), scales=w_scales[:], in_=w_grouped[:]
        )

        x_banks = {}
        x_codes = {}
        x_scales = {}

        def transpose_rows(c):
            x_words = x_raw[c][:].bitcast(F32).rearrange(
                "p (u n i w) -> p u n i w", u=STREAMS, n=CHUNK_UNITS, i=UNIT_TILES
            )
            for n in range(CHUNK_UNITS):
                x_banks[c * CHUNK_UNITS + n] = banks.tile(
                    [P, UNIT_TILES, STREAMS, P], F32, tag="bank", name="x_bank%d%d" % (c, n)
                )
            for u in range(STREAMS):
                for n in range(CHUNK_UNITS):
                    for i in range(UNIT_TILES):
                        nc.tensor.transpose(
                            x_banks[c * CHUNK_UNITS + n][:, i, u, :], x_words[:, u, n, i, :], ident[:]
                        )

        x_grouped = {}

        def group(unit):
            x_grouped[unit] = keep.tile(
                [P, UNIT_ROWS * PACK], BF16, align_bytes=64, name="x_grouped%d" % unit
            )
            nc.scalar.copy(
                out=x_grouped[unit][:].bitcast(F32).rearrange(
                    "p (i r u) -> p i r u", i=UNIT_TILES, u=STREAMS
                ),
                in_=x_banks[unit][:].rearrange("p i u r -> p i r u"),
            )

        def quantise(unit):
            x_codes[unit] = keep.tile([P, UNIT_ROWS], U32, align_bytes=64, name="x_codes%d" % unit)
            x_scales[unit] = keep.tile([P, UNIT_ROWS], U8, align_bytes=64, name="x_scales%d" % unit)
            nc.vector.quantize_mx(
                out=x_codes[unit][:].bitcast(FP8X4),
                scales=x_scales[unit][:],
                in_=x_grouped[unit][:],
            )

        stats = keep.tile([P, O_TILES, UNITS, BN_STATS_DIM], F32)
        y = {}

        def multiply(t, unit):
            o_cols = slice(t * P, (t + 1) * P)
            y[t, unit] = banks.tile([P, UNIT_ROWS], F32, tag="bank", name="y%d%d" % (t, unit))
            nc.tensor.matmul_mx(
                out=y[t, unit][:],
                lhsT=w_codes[:, o_cols].bitcast(FP8X4),
                lhsT_scale=w_scales[:, o_cols],
                rhs=x_codes[unit][:].bitcast(FP8X4),
                rhs_scale=x_scales[unit][:],
                start=True,
                stop=True,
            )

        def sum_up(t, unit):
            nc.vector.bn_stats(out=stats[:, t, unit, :], in_=y[t, unit][:])

        rstd = {}
        neg_mean_gain = {}
        scale = {}
        shift = {}

        def aggregate(t):
            mean_var = keep.tile([P, 2], F32, name="mean_var%d" % t)
            nc.vector.bn_aggr(out=mean_var[:], in_=stats[:, t, :, :].rearrange("p n s -> p (n s)"))
            rstd[t] = keep.tile([P, 1], F32, name="rstd%d" % t)
            nc.scalar.activation(
                out=rstd[t][:], in_=mean_var[:, 1:2], func=ACT.Abs_reciprocal_sqrt, bias=eps[:, 0:1]
            )
            neg_mean_gain[t] = keep.tile([P, 1], F32, name="neg_mean_gain%d" % t)
            nc.vector.tensor_mul(
                out=neg_mean_gain[t][:], in0=mean_var[:, 0:1], in1=neg_gain[:, t : t + 1]
            )

        def scale_and_shift(t):
            scale[t] = keep.tile([P, 1], F32, name="scale%d" % t)
            nc.vector.tensor_mul(out=scale[t][:], in0=rstd[t][:], in1=gain[:, t : t + 1])
            shift[t] = keep.tile([P, 1], F32, name="shift%d" % t)
            nc.vector.tensor_scalar(
                out=shift[t][:],
                in0=neg_mean_gain[t][:],
                scalar1=rstd[t][:],
                scalar2=shift_in[:, t : t + 1],
                op0=ALU.mult,
                op1=ALU.add,
            )

        z = {}
        out_banks = {}

        def normalise(t, unit):
            z[t, unit] = keep.tile([P, UNIT_ROWS], F32, name="z%d%d" % (t, unit))
            if t == 0:
                nc.scalar.activation(
                    out=z[t, unit][:],
                    in_=y[t, unit][:],
                    func=ACT.Identity,
                    scale=scale[t][:],
                    bias=shift[t][:],
                )
            else:
                nc.vector.tensor_scalar(
                    out=z[t, unit][:],
                    in0=y[t, unit][:],
                    scalar1=scale[t][:],
                    scalar2=shift[t][:],
                    op0=ALU.mult,
                    op1=ALU.add,
                )

        def transpose_back(t, unit):
            out_banks[t, unit] = banks.tile(
                [P, UNIT_TILES, P], F32, tag="bank", name="out_bank%d%d" % (t, unit)
            )
            for i in range(UNIT_TILES):
                nc.tensor.transpose(
                    out_banks[t, unit][:, i, :], z[t, unit][:, i * P : (i + 1) * P], ident[:]
                )

        def relu_and_store(t, unit):
            result = keep.tile([P, UNIT_TILES, P], F32, name="result%d%d" % (t, unit))
            nc.scalar.activation(out=result[:], in_=out_banks[t, unit][:], func=ACT.Relu)
            nc.sync.dma_start(
                out=out_rows[:, unit * UNIT_TILES : (unit + 1) * UNIT_TILES, t * P : (t + 1) * P],
                in_=result[:],
            )

        gb_wide = keep.tile([P, P], F32)
        nc.vector.tensor_copy(out=gb_wide[:], in_=gb_rows[:])
        transpose_rows(0)
        gb_bank = banks.tile([P, P], F32, tag="bank")
        nc.tensor.transpose(gb_bank[:], gb_wide[:], ident[:])
        for unit in range(CHUNK_UNITS):
            group(unit)
            quantise(unit)
        gain_shift = keep.tile([P, 2 * O_TILES], F32)
        nc.vector.tensor_copy(out=gain_shift[:], in_=gb_bank[:, 0 : 2 * O_TILES])
        gain = gain_shift[:, 0:O_TILES]
        shift_in = gain_shift[:, O_TILES : 2 * O_TILES]
        neg_gain = keep.tile([P, O_TILES], F32)
        nc.vector.tensor_scalar_mul(out=neg_gain[:], in0=gain, scalar1=-1.0)

        transpose_rows(1)

        for unit in range(CHUNK_UNITS):
            multiply(0, unit)
        for unit in range(CHUNK_UNITS):
            group(CHUNK_UNITS + unit)
            sum_up(0, unit)
            quantise(CHUNK_UNITS + unit)
        for unit in range(CHUNK_UNITS, UNITS):
            multiply(0, unit)
            sum_up(0, unit)
        for unit in range(UNITS):
            multiply(1, unit)
        aggregate(0)
        sum_up(1, 0)
        scale_and_shift(0)
        for unit in range(UNITS):
            normalise(0, unit)
            transpose_back(0, unit)
        for unit in range(1, UNITS):
            sum_up(1, unit)
        aggregate(1)
        scale_and_shift(1)
        for unit in range(UNITS):
            relu_and_store(0, unit)
        for unit in range(UNITS):
            normalise(1, unit)
            transpose_back(1, unit)
            relu_and_store(1, unit)
